import numpy as np
import ml_dtypes


def mxq(x, axis, fmt="e4m3"):
    dtype, down = {"e4m3": (ml_dtypes.float8_e4m3fn, 7), "e5m2": (ml_dtypes.float8_e5m2, 14)}[fmt]
    v = np.moveaxis(np.asarray(x, np.float32).astype(ml_dtypes.bfloat16).astype(np.float64), axis, -1)
    blocks = v.reshape(v.shape[:-1] + (-1, 32))
    amax = np.abs(blocks).max(-1, keepdims=True)
    byte = np.maximum(np.where(amax > 0, np.frexp(amax)[1] - 1 + 127, 0) - down, 1)
    scale = np.exp2(byte - 127.0)
    codes = (blocks / scale).astype(np.float32).astype(dtype).astype(np.float64)
    return np.moveaxis((codes * scale).reshape(v.shape), -1, axis)


WIDE = False


def mx_kscale(k):
    if not WIDE:
        return np.ones(k)
    levels = np.array([10, -10, 5, -5, 0])
    if k % 512:
        return np.exp2(np.random.permutation(np.resize(levels, k // 32))).repeat(32)
    a = np.empty((k // 512, 16))
    for p in range(k // 512):
        a[p, :8] = np.random.permutation(np.resize(levels, 8))
        for g in range(8):
            far = levels[np.abs(levels - a[p, g]) >= 10]
            a[p, g + 8] = far[np.random.randint(len(far))]
    return np.exp2(a.ravel()).repeat(32)


BF16 = ml_dtypes.bfloat16


def bf(x):
    return np.asarray(x, np.float32).astype(BF16)


def f64(x):
    return np.asarray(x).astype(np.float64)


B, S, IQ, OQ, Q = 4, 256, 512, 512, 4


def setup_inputs():
    s = mx_kscale(IQ)
    sw = 0.5 / np.sqrt(IQ)
    return {"x": bf((np.random.standard_normal((B, S, IQ, Q)) * s[:, None]).reshape(B, S, IQ * Q)),
            "wr": bf(np.random.standard_normal((OQ, IQ)) * sw / s),
            "wi": bf(np.random.standard_normal((OQ, IQ)) * sw / s),
            "wj": bf(np.random.standard_normal((OQ, IQ)) * sw / s),
            "wk": bf(np.random.standard_normal((OQ, IQ)) * sw / s),
            "bias": bf(np.random.standard_normal(OQ * Q) * 0.3)}


def core(x, wr, wi, wj, wk, bias):
    xq = f64(x).reshape(B * S, IQ, Q)
    xr = mxq(xq[:, :, 0], 1, "e4m3")
    xi = mxq(xq[:, :, 1], 1, "e4m3")
    xj = mxq(xq[:, :, 2], 1, "e4m3")
    xk = mxq(xq[:, :, 3], 1, "e4m3")
    qr = mxq(f64(wr), 1, "e4m3")
    qi = mxq(f64(wi), 1, "e4m3")
    qj = mxq(f64(wj), 1, "e4m3")
    qk = mxq(f64(wk), 1, "e4m3")
    Ar = xr @ qr.T
    Br = xi @ qr.T
    Cr = xj @ qr.T
    Dr = xk @ qr.T
    Ai = xr @ qi.T
    Bi = xi @ qi.T
    Aj = xr @ qj.T
    Cj = xj @ qj.T
    Ak = xr @ qk.T
    Dk = xk @ qk.T
    or_ = Ar - Bi - Cj - Dk
    oi_ = Br + Ai + Dk - Cj
    oj_ = Cr - Dk + Aj + Bi
    ok_ = Dr + Cj - Bi + Ak
    out = np.stack([or_, oi_, oj_, ok_], axis=-1).reshape(B, S, Q * OQ)
    return out + f64(bias)[None, None, :]


def e4m3fn_bytes(y):
    return np.clip(np.asarray(y, np.float64), -448.0, 448.0).astype(np.float32).astype(ml_dtypes.float8_e4m3fn).view(np.uint8)


Y_SCALE = 210.0


def reference(x, wr, wi, wj, wk, bias):
    out = core(x, wr, wi, wj, wk, bias)
    return out, e4m3fn_bytes(out * Y_SCALE)

@@ -1,0 +1,200 @@
+from contextlib import ExitStack
+
+import concourse.mybir as mybir
+from concourse.masks import make_identity
+
+FLOPS = 10 * 2 * 1024 * 512 * 512
+
+F32 = mybir.dt.float32
+BF16 = mybir.dt.bfloat16
+U32 = mybir.dt.uint32
+U8 = mybir.dt.uint8
+FP8X4 = mybir.dt.float8_e4m3fn_x4
+FP8 = mybir.dt.float8_e4m3fn
+ACT = mybir.ActivationFunctionType
+ALU = mybir.AluOpType
+
+P = 128
+ROW_TILES = 8
+O_BLOCKS = 4
+Y_SCALE = 210.0
+
+SEQ = ((-1, 3), (1, 0), (1, 1), (-1, 1), (1, 0), (1, 2), (1, 3), (-1, 3), (1, 3), (-1, 2), (-1, 2))
+WIN = ((1, 5), (3, 2), (9, 4), (7, 0))
+QCALLS = ((1, 2), (3, 1), (4, 1), (9, 1), (10, 1), (7, 1), (8, 1), (5, 2), (0, 1))
+
+
+def tile_quaternionlinear_pa_kernel(tc, x, wr, wi, wj, wk, bias, out_0, out_1):
+    nc = tc.nc
+    xf = x.flatten_outer_dims()
+    o0 = out_0.flatten_outer_dims()
+    o1 = out_1.flatten_outer_dims()
+    weights = (wr, wi, wj, wk)
+
+    with ExitStack() as ctx:
+        const = ctx.enter_context(tc.tile_pool(name="const", bufs=1))
+        gxp = ctx.enter_context(tc.tile_pool(name="gxp", bufs=3))
+        outp = ctx.enter_context(tc.tile_pool(name="outp", bufs=4))
+        tp = ctx.enter_context(tc.psum_pool(name="tp", bufs=4))
+        accp = ctx.enter_context(tc.psum_pool(name="accp", bufs=4))
+
+        ones = const.tile([P, P], BF16, name="ones")
+        nc.vector.memset(ones[:], 1.0)
+        brow = const.tile([P, 2048], BF16, name="brow")
+        nc.vector.memset(brow[:], 0.0)
+        nc.scalar.dma_start(out=brow[0:1, :], in_=bias.rearrange("(a n) -> a n", a=1))
+        warm = const.tile([P, 1], F32, name="warm")
+        nc.scalar.activation(out=warm[:], in_=ones[:, 0:1], func=ACT.Copy)
+        ident = const.tile([P, P], F32, name="ident")
+        make_identity(nc, ident[:])
+        bias_sb = const.tile([P, 2048], F32, name="bias_sb")
+
+        wraw = []
+        for w in range(4):
+            wraw.append([const.tile([P, 512], BF16, name="wraw%d_%d" % (w, b)) for b in range(O_BLOCKS)])
+        xraw = [const.tile([P, 2048], BF16, name="xraw%d" % r) for r in range(ROW_TILES)]
+        gw = [const.tile([P, 4, P, 4], BF16, name="gw%d" % b, align_bytes=64) for b in range(O_BLOCKS)]
+        gn = [const.tile([P, 3, P, 4], BF16, name="gn%d" % b, align_bytes=64) for b in range(O_BLOCKS)]
+        wc = [const.tile([P, 11 * P], U32, name="wc%d" % b, align_bytes=64) for b in range(O_BLOCKS)]
+        ws = [const.tile([P, 11 * P], U8, name="ws%d" % b, align_bytes=64) for b in range(O_BLOCKS)]
+        xc = [const.tile([P, 4 * P], U32, name="xc%d" % r, align_bytes=64) for r in range(ROW_TILES)]
+        xs = [const.tile([P, 4 * P], U8, name="xs%d" % r, align_bytes=64) for r in range(ROW_TILES)]
+
+        def load_w(b):
+            for w in range(4):
+                nc.sync.dma_start(out=wraw[w][b][:], in_=weights[w][P * b:P * (b + 1), :])
+
+        def load_x(r):
+            nc.sync.dma_start(out=xraw[r][:], in_=xf[P * r:P * (r + 1), :])
+
+        load_w(0)
+        load_x(0)
+        load_x(1)
+        load_w(1)
+        load_w(2)
+        load_w(3)
+        for r in range(2, ROW_TILES):
+            load_x(r)
+
+        def w_transpose(b):
+            for half in range(2):
+                wt = tp.tile([P, 2, 2, P], F32, name="wt", tag="tp")
+                for w2 in range(2):
+                    words = wraw[2 * half + w2][b][:].bitcast(F32)
+                    for u in range(2):
+                        nc.tensor.transpose(wt[:, w2, u, :], words[:, u:256:2], ident[:])
+                nc.scalar.copy(
+                    out=gw[b][:, 2 * half:2 * half + 2, :, :].bitcast(F32),
+                    in_=wt[:].rearrange("p w u j -> p w j u"),
+                )
+
+        def w_quant(b):
+            nc.vector.tensor_scalar(out=gn[b][:], in0=gw[b][:, 1:4, :, :], scalar1=-1.0, scalar2=None, op0=ALU.mult)
+            pos = gw[b][:].rearrange("p w j t -> p (w j t)")
+            neg = gn[b][:].rearrange("p w j t -> p (w j t)")
+            for first, count in QCALLS:
+                sign, w = SEQ[first]
+                if sign > 0:
+                    src = pos[:, 512 * w:512 * (w + count)]
+                else:
+                    src = neg[:, 512 * (w - 1):512 * (w - 1 + count)]
+                cols = slice(P * first, P * (first + count))
+                nc.vector.quantize_mx(out=wc[b][:, cols].bitcast(FP8X4), scales=ws[b][:, cols], in_=src)
+
+        gx_of = {}
+
+        def x_transpose(r):
+            words = xraw[r][:].bitcast(F32)
+            gx = gxp.tile([P, 4, P, 4], BF16, name="gx", align_bytes=64)
+            gx_of[r] = gx
+            for h in range(2):
+                xt = tp.tile([P, 4, P], F32, name="xt", tag="tp")
+                for t in range(4):
+                    nc.tensor.transpose(xt[:, t, :], words[:, 2 * t + h:1024:8], ident[:])
+                nc.scalar.copy(
+                    out=gx[:, 2 * h:2 * h + 2, :, :],
+                    in_=xt[:].bitcast(BF16).rearrange("p t (n e) -> p e n t", e=2),
+                )
+
+        def x_quant(r):
+            nc.vector.quantize_mx(
+                out=xc[r][:].bitcast(FP8X4),
+                scales=xs[r][:],
+                in_=gx_of[r][:].rearrange("p c n t -> p (c n t)"),
+            )
+
+        def bias_setup():
+            for q in range(4):
+                bp = tp.tile([P, 512], F32, name="bp", tag="tp")
+                nc.tensor.matmul(out=bp[:], lhsT=ones[:], rhs=brow[:, 512 * q:512 * (q + 1)], start=True, stop=True)
+                nc.vector.tensor_copy(out=bias_sb[:, 512 * q:512 * (q + 1)], in_=bp[:])
+
+        res_of = {}
+
+        def job(r, b):
+            if b == 0:
+                res = outp.tile([P, 2048], F32, name="res")
+                f8 = outp.tile([P, 2048], FP8, name="f8")
+                res_of[r] = (res, f8)
+            res, f8 = res_of[r]
+            acc = accp.tile([P, 512], F32, name="acc")
+            for cp in range(2):
+                for a in range(4):
+                    wcols = slice(P * WIN[a][cp], P * (WIN[a][cp] + 2))
+                    xcols = slice(P * a, P * (a + 1))
+                    nc.tensor.matmul_mx(
+                        out=acc[:, 256 * cp:256 * (cp + 1)],
+                        lhsT=xc[r][:, xcols].bitcast(FP8X4),
+                        lhsT_scale=xs[r][:, xcols],
+                        rhs=wc[b][:, wcols].bitcast(FP8X4),
+                        rhs_scale=ws[b][:, wcols],
+                        start=(a == 0),
+                        stop=(a == 3),
+                    )
+            cols = slice(512 * b, 512 * (b + 1))
+            nc.vector.tensor_tensor(
+                out=res[:, cols].rearrange("p (j c) -> p j c", c=4),
+                in0=acc[:].rearrange("p (c j) -> p j c", c=4),
+                in1=bias_sb[:, cols].rearrange("p (j c) -> p j c", c=4),
+                op=ALU.add,
+            )
+            nc.scalar.activation(out=f8[:, cols], in_=res[:, cols], func=ACT.Copy, scale=Y_SCALE, saturate=False)
+            if b % 2 == 1:
+                rows = slice(P * r, P * (r + 1))
+                half = slice(512 * (b - 1), 512 * (b + 1))
+                nc.sync.dma_start(out=o0[rows, half], in_=res[:, half])
+                nc.sync.dma_start(out=o1[rows, half], in_=f8[:, half].bitcast(U8))
+
+        with tc.manual_schedule(engines={mybir.EngineType.PE}):
+            w_transpose(0)
+            x_transpose(0)
+            w_quant(0)
+            x_quant(0)
+            x_transpose(1)
+            w_transpose(1)
+            bias_setup()
+            x_quant(1)
+            w_quant(1)
+            job(0, 0)
+            job(1, 0)
+            w_transpose(2)
+            x_transpose(2)
+            w_quant(2)
+            job(0, 1)
+            job(1, 1)
+            w_transpose(3)
+            x_quant(2)
+            w_quant(3)
+            job(0, 2)
+            job(1, 2)
+            x_transpose(3)
+            job(0, 3)
+            job(1, 3)
+            x_quant(3)
+            for r in range(2, ROW_TILES):
+                if r + 2 < ROW_TILES:
+                    x_transpose(r + 2)
+                for b in range(O_BLOCKS):
+                    job(r, b)
+                if r + 2 < ROW_TILES:
+                    x_quant(r + 2)

@@ -22,6 +22,8 @@ Y_SCALE = 210.0
 SEQ = ((-1, 3), (1, 0), (1, 1), (-1, 1), (1, 0), (1, 2), (1, 3), (-1, 3), (1, 3), (-1, 2), (-1, 2))
 WIN = ((1, 5), (3, 2), (9, 4), (7, 0))
 QCALLS = ((1, 2), (3, 1), (4, 1), (9, 1), (10, 1), (7, 1), (8, 1), (5, 2), (0, 1))
+ORDER = (("w", 0), ("x", 0), ("w", 1), ("x", 1), ("x", 2), ("w", 2), ("x", 3), ("x", 4), ("w", 3), ("x", 5), ("x", 6), ("x", 7))
+V_COPIES = (0, 1, 2, 3, 4, 5, 6, 7)
 
 
 def tile_quaternionlinear_pa_kernel(tc, x, wr, wi, wj, wk, bias, out_0, out_1):
@@ -33,52 +35,40 @@ def tile_quaternionlinear_pa_kernel(tc, x, wr, wi, wj, wk, bias, out_0, out_1):
 
     with ExitStack() as ctx:
         const = ctx.enter_context(tc.tile_pool(name="const", bufs=1))
-        gxp = ctx.enter_context(tc.tile_pool(name="gxp", bufs=3))
-        outp = ctx.enter_context(tc.tile_pool(name="outp", bufs=4))
-        tp = ctx.enter_context(tc.psum_pool(name="tp", bufs=4))
-        accp = ctx.enter_context(tc.psum_pool(name="accp", bufs=4))
+        share = ctx.enter_context(tc.tile_pool(name="share", bufs=1))
+        outp = ctx.enter_context(tc.tile_pool(name="outp", bufs=8))
+        ps = ctx.enter_context(tc.psum_pool(name="ps", bufs=8))
 
-        ones = const.tile([P, P], BF16, name="ones")
-        nc.vector.memset(ones[:], 1.0)
-        brow = const.tile([P, 2048], BF16, name="brow")
-        nc.vector.memset(brow[:], 0.0)
-        nc.scalar.dma_start(out=brow[0:1, :], in_=bias.rearrange("(a n) -> a n", a=1))
+        one = const.tile([P, 1], F32, name="one")
+        nc.vector.memset(one[:], 1.0)
         warm = const.tile([P, 1], F32, name="warm")
-        nc.scalar.activation(out=warm[:], in_=ones[:, 0:1], func=ACT.Copy)
+        nc.scalar.activation(out=warm[:], in_=one[:], func=ACT.Copy)
         ident = const.tile([P, P], F32, name="ident")
         make_identity(nc, ident[:])
-        bias_sb = const.tile([P, 2048], F32, name="bias_sb")
 
         wraw = []
         for w in range(4):
             wraw.append([const.tile([P, 512], BF16, name="wraw%d_%d" % (w, b)) for b in range(O_BLOCKS)])
-        xraw = [const.tile([P, 2048], BF16, name="xraw%d" % r) for r in range(ROW_TILES)]
+        xraw = [const.tile([P, 2048], BF16, name="xraw%d" % r) for r in range(ROW_TILES - 1)]
+        xraw.append(share.tile([P, 2048], BF16, name="xraw7", tag="slot"))
         gw = [const.tile([P, 4, P, 4], BF16, name="gw%d" % b, align_bytes=64) for b in range(O_BLOCKS)]
         gn = [const.tile([P, 3, P, 4], BF16, name="gn%d" % b, align_bytes=64) for b in range(O_BLOCKS)]
+        gx = [const.tile([P, 4, P, 4], BF16, name="gx%d" % r, align_bytes=64) for r in range(ROW_TILES)]
         wc = [const.tile([P, 11 * P], U32, name="wc%d" % b, align_bytes=64) for b in range(O_BLOCKS)]
         ws = [const.tile([P, 11 * P], U8, name="ws%d" % b, align_bytes=64) for b in range(O_BLOCKS)]
         xc = [const.tile([P, 4 * P], U32, name="xc%d" % r, align_bytes=64) for r in range(ROW_TILES)]
         xs = [const.tile([P, 4 * P], U8, name="xs%d" % r, align_bytes=64) for r in range(ROW_TILES)]
 
-        def load_w(b):
-            for w in range(4):
-                nc.sync.dma_start(out=wraw[w][b][:], in_=weights[w][P * b:P * (b + 1), :])
-
-        def load_x(r):
-            nc.sync.dma_start(out=xraw[r][:], in_=xf[P * r:P * (r + 1), :])
-
-        load_w(0)
-        load_x(0)
-        load_x(1)
-        load_w(1)
-        load_w(2)
-        load_w(3)
-        for r in range(2, ROW_TILES):
-            load_x(r)
+        for kind, idx in ORDER:
+            if kind == "w":
+                for w in range(4):
+                    nc.sync.dma_start(out=wraw[w][idx][:], in_=weights[w][P * idx:P * (idx + 1), :])
+            else:
+                nc.sync.dma_start(out=xraw[idx][:], in_=xf[P * idx:P * (idx + 1), :])
 
         def w_transpose(b):
             for half in range(2):
-                wt = tp.tile([P, 2, 2, P], F32, name="wt", tag="tp")
+                wt = ps.tile([P, 2, 2, P], F32, name="wt", tag="bank")
                 for w2 in range(2):
                     words = wraw[2 * half + w2][b][:].bitcast(F32)
                     for u in range(2):
@@ -101,43 +91,27 @@ def tile_quaternionlinear_pa_kernel(tc, x, wr, wi, wj, wk, bias, out_0, out_1):
                 cols = slice(P * first, P * (first + count))
                 nc.vector.quantize_mx(out=wc[b][:, cols].bitcast(FP8X4), scales=ws[b][:, cols], in_=src)
 
-        gx_of = {}
-
         def x_transpose(r):
             words = xraw[r][:].bitcast(F32)
-            gx = gxp.tile([P, 4, P, 4], BF16, name="gx", align_bytes=64)
-            gx_of[r] = gx
             for h in range(2):
-                xt = tp.tile([P, 4, P], F32, name="xt", tag="tp")
+                xt = ps.tile([P, 4, P], F32, name="xt", tag="bank")
                 for t in range(4):
                     nc.tensor.transpose(xt[:, t, :], words[:, 2 * t + h:1024:8], ident[:])
-                nc.scalar.copy(
-                    out=gx[:, 2 * h:2 * h + 2, :, :],
-                    in_=xt[:].bitcast(BF16).rearrange("p t (n e) -> p e n t", e=2),
-                )
+                parted = xt[:].bitcast(BF16).rearrange("p t (n e) -> p e n t", e=2)
+                if h == 1 and r in V_COPIES:
+                    nc.vector.tensor_copy(out=gx[r][:, 2 * h:2 * h + 2, :, :], in_=parted)
+                else:
+                    nc.scalar.copy(out=gx[r][:, 2 * h:2 * h + 2, :, :], in_=parted)
 
         def x_quant(r):
             nc.vector.quantize_mx(
                 out=xc[r][:].bitcast(FP8X4),
                 scales=xs[r][:],
-                in_=gx_of[r][:].rearrange("p c n t -> p (c n t)"),
+                in_=gx[r][:].rearrange("p c n t -> p (c n t)"),
             )
 
-        def bias_setup():
-            for q in range(4):
-                bp = tp.tile([P, 512], F32, name="bp", tag="tp")
-                nc.tensor.matmul(out=bp[:], lhsT=ones[:], rhs=brow[:, 512 * q:512 * (q + 1)], start=True, stop=True)
-                nc.vector.tensor_copy(out=bias_sb[:, 512 * q:512 * (q + 1)], in_=bp[:])
-
-        res_of = {}
-
-        def job(r, b):
-            if b == 0:
-                res = outp.tile([P, 2048], F32, name="res")
-                f8 = outp.tile([P, 2048], FP8, name="f8")
-                res_of[r] = (res, f8)
-            res, f8 = res_of[r]
-            acc = accp.tile([P, 512], F32, name="acc")
+        def job(r, b, bias_sb):
+            acc = ps.tile([P, 512], F32, name="acc", tag="bank")
             for cp in range(2):
                 for a in range(4):
                     wcols = slice(P * WIN[a][cp], P * (WIN[a][cp] + 2))
@@ -152,49 +126,35 @@ def tile_quaternionlinear_pa_kernel(tc, x, wr, wi, wj, wk, bias, out_0, out_1):
                         stop=(a == 3),
                     )
             cols = slice(512 * b, 512 * (b + 1))
+            rows = slice(P * r, P * (r + 1))
+            res = outp.tile([P, 512], F32, name="res")
+            f8 = outp.tile([P, 512], FP8, name="f8")
             nc.vector.tensor_tensor(
-                out=res[:, cols].rearrange("p (j c) -> p j c", c=4),
+                out=res[:].rearrange("p (j c) -> p j c", c=4),
                 in0=acc[:].rearrange("p (c j) -> p j c", c=4),
                 in1=bias_sb[:, cols].rearrange("p (j c) -> p j c", c=4),
                 op=ALU.add,
             )
-            nc.scalar.activation(out=f8[:, cols], in_=res[:, cols], func=ACT.Copy, scale=Y_SCALE, saturate=False)
-            if b % 2 == 1:
-                rows = slice(P * r, P * (r + 1))
-                half = slice(512 * (b - 1), 512 * (b + 1))
-                nc.sync.dma_start(out=o0[rows, half], in_=res[:, half])
-                nc.sync.dma_start(out=o1[rows, half], in_=f8[:, half].bitcast(U8))
+            nc.sync.dma_start(out=o0[rows, cols], in_=res[:])
+            nc.scalar.activation(out=f8[:], in_=res[:], func=ACT.Copy, scale=Y_SCALE, saturate=False)
+            nc.sync.dma_start(out=o1[rows, cols], in_=f8[:].bitcast(U8))
 
         with tc.manual_schedule(engines={mybir.EngineType.PE}):
-            w_transpose(0)
-            x_transpose(0)
-            w_quant(0)
-            x_quant(0)
-            x_transpose(1)
-            w_transpose(1)
-            bias_setup()
-            x_quant(1)
-            w_quant(1)
-            job(0, 0)
-            job(1, 0)
-            w_transpose(2)
-            x_transpose(2)
-            w_quant(2)
-            job(0, 1)
-            job(1, 1)
-            w_transpose(3)
-            x_quant(2)
-            w_quant(3)
-            job(0, 2)
-            job(1, 2)
-            x_transpose(3)
-            job(0, 3)
-            job(1, 3)
-            x_quant(3)
-            for r in range(2, ROW_TILES):
-                if r + 2 < ROW_TILES:
-                    x_transpose(r + 2)
-                for b in range(O_BLOCKS):
-                    job(r, b)
-                if r + 2 < ROW_TILES:
-                    x_quant(r + 2)
+            for kind, idx in ORDER:
+                if kind == "w":
+                    w_transpose(idx)
+                    if idx == 0:
+                        w_quant(0)
+                else:
+                    x_transpose(idx)
+                    if idx == 0:
+                        x_quant(0)
+            bias_sb = share.tile([P, 2048], BF16, name="bias_sb", tag="slot")
+            nc.sync.dma_start(out=bias_sb[:], in_=bias.partition_broadcast(P))
+            for r in range(1, ROW_TILES):
+                x_quant(r)
+            for b in range(O_BLOCKS):
+                if b + 1 < O_BLOCKS:
+                    w_quant(b + 1)
+                for r in range(ROW_TILES):
+                    job(r, b, bias_sb)

@@ -36,7 +36,7 @@ def tile_quaternionlinear_pa_kernel(tc, x, wr, wi, wj, wk, bias, out_0, out_1):
     with ExitStack() as ctx:
         const = ctx.enter_context(tc.tile_pool(name="const", bufs=1))
         share = ctx.enter_context(tc.tile_pool(name="share", bufs=1))
-        outp = ctx.enter_context(tc.tile_pool(name="outp", bufs=8))
+        outp = ctx.enter_context(tc.tile_pool(name="outp", bufs=6))
         ps = ctx.enter_context(tc.psum_pool(name="ps", bufs=8))
 
         one = const.tile([P, 1], F32, name="one")
@@ -110,7 +110,14 @@ def tile_quaternionlinear_pa_kernel(tc, x, wr, wi, wj, wk, bias, out_0, out_1):
                 in_=gx[r][:].rearrange("p c n t -> p (c n t)"),
             )
 
+        res_of = {}
+
         def job(r, b, bias_sb):
+            if b % 2 == 0:
+                res = outp.tile([P, 1024], F32, name="res")
+                f8 = outp.tile([P, 1024], FP8, name="f8")
+                res_of[r] = (res, f8)
+            res, f8 = res_of[r]
             acc = ps.tile([P, 512], F32, name="acc", tag="bank")
             for cp in range(2):
                 for a in range(4):
@@ -126,18 +133,19 @@ def tile_quaternionlinear_pa_kernel(tc, x, wr, wi, wj, wk, bias, out_0, out_1):
                         stop=(a == 3),
                     )
             cols = slice(512 * b, 512 * (b + 1))
-            rows = slice(P * r, P * (r + 1))
-            res = outp.tile([P, 512], F32, name="res")
-            f8 = outp.tile([P, 512], FP8, name="f8")
+            part = slice(512 * (b % 2), 512 * (b % 2 + 1))
             nc.vector.tensor_tensor(
-                out=res[:].rearrange("p (j c) -> p j c", c=4),
+                out=res[:, part].rearrange("p (j c) -> p j c", c=4),
                 in0=acc[:].rearrange("p (c j) -> p j c", c=4),
                 in1=bias_sb[:, cols].rearrange("p (j c) -> p j c", c=4),
                 op=ALU.add,
             )
-            nc.sync.dma_start(out=o0[rows, cols], in_=res[:])
-            nc.scalar.activation(out=f8[:], in_=res[:], func=ACT.Copy, scale=Y_SCALE, saturate=False)
-            nc.sync.dma_start(out=o1[rows, cols], in_=f8[:].bitcast(U8))
+            nc.scalar.activation(out=f8[:, part], in_=res[:, part], func=ACT.Copy, scale=Y_SCALE, saturate=False)
+            if b % 2 == 1:
+                rows = slice(P * r, P * (r + 1))
+                half = slice(512 * (b - 1), 512 * (b + 1))
+                nc.sync.dma_start(out=o0[rows, half], in_=res[:])
+                nc.sync.dma_start(out=o1[rows, half], in_=f8[:].bitcast(U8))
 
         with tc.manual_schedule(engines={mybir.EngineType.PE}):
             for kind, idx in ORDER:
@@ -149,12 +157,17 @@ def tile_quaternionlinear_pa_kernel(tc, x, wr, wi, wj, wk, bias, out_0, out_1):
                     x_transpose(idx)
                     if idx == 0:
                         x_quant(0)
+                    if idx == 2:
+                        w_quant(1)
             bias_sb = share.tile([P, 2048], BF16, name="bias_sb", tag="slot")
             nc.sync.dma_start(out=bias_sb[:], in_=bias.partition_broadcast(P))
             for r in range(1, ROW_TILES):
                 x_quant(r)
-            for b in range(O_BLOCKS):
-                if b + 1 < O_BLOCKS:
-                    w_quant(b + 1)
+            for pair in range(2):
                 for r in range(ROW_TILES):
-                    job(r, b, bias_sb)
+                    if pair == 0 and r == 2:
+                        w_quant(2)
+                    if pair == 0 and r == 5:
+                        w_quant(3)
+                    job(r, 2 * pair, bias_sb)
+                    job(r, 2 * pair + 1, bias_sb)

@@ -23,7 +23,7 @@ SEQ = ((-1, 3), (1, 0), (1, 1), (-1, 1), (1, 0), (1, 2), (1, 3), (-1, 3), (1, 3)
 WIN = ((1, 5), (3, 2), (9, 4), (7, 0))
 QCALLS = ((1, 2), (3, 1), (4, 1), (9, 1), (10, 1), (7, 1), (8, 1), (5, 2), (0, 1))
 ORDER = (("w", 0), ("x", 0), ("w", 1), ("x", 1), ("x", 2), ("w", 2), ("x", 3), ("x", 4), ("w", 3), ("x", 5), ("x", 6), ("x", 7))
-V_COPIES = (0, 1, 2, 3, 4, 5, 6, 7)
+V_COPIES = (0, 1, 2, 3)
 
 
 def tile_quaternionlinear_pa_kernel(tc, x, wr, wi, wj, wk, bias, out_0, out_1):

@@ -22,7 +22,7 @@ Y_SCALE = 210.0
 SEQ = ((-1, 3), (1, 0), (1, 1), (-1, 1), (1, 0), (1, 2), (1, 3), (-1, 3), (1, 3), (-1, 2), (-1, 2))
 WIN = ((1, 5), (3, 2), (9, 4), (7, 0))
 QCALLS = ((1, 2), (3, 1), (4, 1), (9, 1), (10, 1), (7, 1), (8, 1), (5, 2), (0, 1))
-ORDER = (("w", 0), ("x", 0), ("w", 1), ("x", 1), ("x", 2), ("w", 2), ("x", 3), ("x", 4), ("w", 3), ("x", 5), ("x", 6), ("x", 7))
+ORDER = (("w", 0), ("w", 1), ("w", 2), ("w", 3), ("x", 0), ("x", 1), ("x", 2), ("x", 3), ("x", 4), ("x", 5), ("x", 6), ("x", 7))
 V_COPIES = (0, 1, 2, 3)
 
 
@@ -46,12 +46,11 @@ def tile_quaternionlinear_pa_kernel(tc, x, wr, wi, wj, wk, bias, out_0, out_1):
         ident = const.tile([P, P], F32, name="ident")
         make_identity(nc, ident[:])
 
-        wraw = []
-        for w in range(4):
-            wraw.append([const.tile([P, 512], BF16, name="wraw%d_%d" % (w, b)) for b in range(O_BLOCKS)])
+        wraw = [const.tile([P, O_BLOCKS, 512], BF16, name="wraw%d" % w) for w in range(4)]
         xraw = [const.tile([P, 2048], BF16, name="xraw%d" % r) for r in range(ROW_TILES - 1)]
         xraw.append(share.tile([P, 2048], BF16, name="xraw7", tag="slot"))
-        gw = [const.tile([P, 4, P, 4], BF16, name="gw%d" % b, align_bytes=64) for b in range(O_BLOCKS)]
+        gwall = const.tile([P, O_BLOCKS, 4, P, 4], BF16, name="gwall", align_bytes=64)
+        gw = [gwall[:, b, :, :, :] for b in range(O_BLOCKS)]
         gn = [const.tile([P, 3, P, 4], BF16, name="gn%d" % b, align_bytes=64) for b in range(O_BLOCKS)]
         gx = [const.tile([P, 4, P, 4], BF16, name="gx%d" % r, align_bytes=64) for r in range(ROW_TILES)]
         wc = [const.tile([P, 11 * P], U32, name="wc%d" % b, align_bytes=64) for b in range(O_BLOCKS)]
@@ -59,28 +58,28 @@ def tile_quaternionlinear_pa_kernel(tc, x, wr, wi, wj, wk, bias, out_0, out_1):
         xc = [const.tile([P, 4 * P], U32, name="xc%d" % r, align_bytes=64) for r in range(ROW_TILES)]
         xs = [const.tile([P, 4 * P], U8, name="xs%d" % r, align_bytes=64) for r in range(ROW_TILES)]
 
-        for kind, idx in ORDER:
-            if kind == "w":
-                for w in range(4):
-                    nc.sync.dma_start(out=wraw[w][idx][:], in_=weights[w][P * idx:P * (idx + 1), :])
-            else:
-                nc.sync.dma_start(out=xraw[idx][:], in_=xf[P * idx:P * (idx + 1), :])
+        queues = (nc.sync, nc.scalar)
+        for w in range(4):
+            queues[w % 2].dma_start(out=wraw[w][:], in_=weights[w].rearrange("(b p) k -> p b k", b=O_BLOCKS))
+        for r in range(ROW_TILES):
+            queue = queues[r % 2] if r < 4 else nc.sync
+            queue.dma_start(out=xraw[r][:], in_=xf[P * r:P * (r + 1), :])
 
-        def w_transpose(b):
+        def w_transpose(w):
             for half in range(2):
                 wt = ps.tile([P, 2, 2, P], F32, name="wt", tag="bank")
-                for w2 in range(2):
-                    words = wraw[2 * half + w2][b][:].bitcast(F32)
+                for b2 in range(2):
+                    words = wraw[w][:, 2 * half + b2, :].bitcast(F32)
                     for u in range(2):
-                        nc.tensor.transpose(wt[:, w2, u, :], words[:, u:256:2], ident[:])
+                        nc.tensor.transpose(wt[:, b2, u, :], words[:, u:256:2], ident[:])
                 nc.scalar.copy(
-                    out=gw[b][:, 2 * half:2 * half + 2, :, :].bitcast(F32),
-                    in_=wt[:].rearrange("p w u j -> p w j u"),
+                    out=gwall[:, 2 * half:2 * half + 2, w, :, :].bitcast(F32),
+                    in_=wt[:].rearrange("p b u j -> p b j u"),
                 )
 
         def w_quant(b):
             nc.vector.tensor_scalar(out=gn[b][:], in0=gw[b][:, 1:4, :, :], scalar1=-1.0, scalar2=None, op0=ALU.mult)
-            pos = gw[b][:].rearrange("p w j t -> p (w j t)")
+            pos = gw[b].rearrange("p w j t -> p (w j t)")
             neg = gn[b][:].rearrange("p w j t -> p (w j t)")
             for first, count in QCALLS:
                 sign, w = SEQ[first]
@@ -144,21 +143,20 @@ def tile_quaternionlinear_pa_kernel(tc, x, wr, wi, wj, wk, bias, out_0, out_1):
             if b % 2 == 1:
                 rows = slice(P * r, P * (r + 1))
                 half = slice(512 * (b - 1), 512 * (b + 1))
-                nc.sync.dma_start(out=o0[rows, half], in_=res[:])
+                nc.scalar.dma_start(out=o0[rows, half], in_=res[:])
                 nc.sync.dma_start(out=o1[rows, half], in_=f8[:].bitcast(U8))
 
         with tc.manual_schedule(engines={mybir.EngineType.PE}):
             for kind, idx in ORDER:
                 if kind == "w":
                     w_transpose(idx)
-                    if idx == 0:
+                    if idx == 3:
                         w_quant(0)
+                        w_quant(1)
                 else:
                     x_transpose(idx)
                     if idx == 0:
                         x_quant(0)
-                    if idx == 2:
-                        w_quant(1)
             bias_sb = share.tile([P, 2048], BF16, name="bias_sb", tag="slot")
             nc.sync.dma_start(out=bias_sb[:], in_=bias.partition_broadcast(P))
             for r in range(1, ROW_TILES):

from contextlib import ExitStack

import concourse.mybir as mybir
from concourse.masks import make_identity

FLOPS = 10 * 2 * 1024 * 512 * 512

F32 = mybir.dt.float32
BF16 = mybir.dt.bfloat16
U32 = mybir.dt.uint32
U8 = mybir.dt.uint8
FP8X4 = mybir.dt.float8_e4m3fn_x4
FP8 = mybir.dt.float8_e4m3fn
ACT = mybir.ActivationFunctionType
ALU = mybir.AluOpType

P = 128
ROW_TILES = 8
O_BLOCKS = 4
Y_SCALE = 210.0

SEQ = ((-1, 3), (1, 0), (1, 1), (-1, 1), (1, 0), (1, 2), (1, 3), (-1, 3), (1, 3), (-1, 2), (-1, 2))
WIN = ((1, 5), (3, 2), (9, 4), (7, 0))
QCALLS = ((1, 2), (3, 1), (4, 1), (9, 1), (10, 1), (7, 1), (8, 1), (5, 2), (0, 1))
ORDER = (("w", 0), ("w", 1), ("w", 2), ("w", 3), ("x", 0), ("x", 1), ("x", 2), ("x", 3), ("x", 4), ("x", 5), ("x", 6), ("x", 7))
V_COPIES = (0, 1, 2, 3)


def tile_quaternionlinear_pa_kernel(tc, x, wr, wi, wj, wk, bias, out_0, out_1):
    nc = tc.nc
    xf = x.flatten_outer_dims()
    o0 = out_0.flatten_outer_dims()
    o1 = out_1.flatten_outer_dims()
    weights = (wr, wi, wj, wk)

    with ExitStack() as ctx:
        const = ctx.enter_context(tc.tile_pool(name="const", bufs=1))
        share = ctx.enter_context(tc.tile_pool(name="share", bufs=1))
        outp = ctx.enter_context(tc.tile_pool(name="outp", bufs=6))
        ps = ctx.enter_context(tc.psum_pool(name="ps", bufs=8))

        one = const.tile([P, 1], F32, name="one")
        nc.vector.memset(one[:], 1.0)
        warm = const.tile([P, 1], F32, name="warm")
        nc.scalar.activation(out=warm[:], in_=one[:], func=ACT.Copy)
        ident = const.tile([P, P], F32, name="ident")
        make_identity(nc, ident[:])

        wraw = [const.tile([P, O_BLOCKS, 512], BF16, name="wraw%d" % w) for w in range(4)]
        xraw = [const.tile([P, 2048], BF16, name="xraw%d" % r) for r in range(ROW_TILES - 1)]
        xraw.append(share.tile([P, 2048], BF16, name="xraw7", tag="slot"))
        gwall = const.tile([P, O_BLOCKS, 4, P, 4], BF16, name="gwall", align_bytes=64)
        gw = [gwall[:, b, :, :, :] for b in range(O_BLOCKS)]
        gn = [const.tile([P, 3, P, 4], BF16, name="gn%d" % b, align_bytes=64) for b in range(O_BLOCKS)]
        gx = [const.tile([P, 4, P, 4], BF16, name="gx%d" % r, align_bytes=64) for r in range(ROW_TILES)]
        wc = [const.tile([P, 11 * P], U32, name="wc%d" % b, align_bytes=64) for b in range(O_BLOCKS)]
        ws = [const.tile([P, 11 * P], U8, name="ws%d" % b, align_bytes=64) for b in range(O_BLOCKS)]
        xc = [const.tile([P, 4 * P], U32, name="xc%d" % r, align_bytes=64) for r in range(ROW_TILES)]
        xs = [const.tile([P, 4 * P], U8, name="xs%d" % r, align_bytes=64) for r in range(ROW_TILES)]

        queues = (nc.sync, nc.scalar)
        for w in range(4):
            queues[w % 2].dma_start(out=wraw[w][:], in_=weights[w].rearrange("(b p) k -> p b k", b=O_BLOCKS))
        for r in range(ROW_TILES):
            queue = queues[r % 2] if r < 4 else nc.sync
            queue.dma_start(out=xraw[r][:], in_=xf[P * r:P * (r + 1), :])

        def w_transpose(w):
            for half in range(2):
                wt = ps.tile([P, 2, 2, P], F32, name="wt", tag="bank")
                for b2 in range(2):
                    words = wraw[w][:, 2 * half + b2, :].bitcast(F32)
                    for u in range(2):
                        nc.tensor.transpose(wt[:, b2, u, :], words[:, u:256:2], ident[:])
                nc.scalar.copy(
                    out=gwall[:, 2 * half:2 * half + 2, w, :, :].bitcast(F32),
                    in_=wt[:].rearrange("p b u j -> p b j u"),
                )

        def w_quant(b):
            nc.vector.tensor_scalar(out=gn[b][:], in0=gw[b][:, 1:4, :, :], scalar1=-1.0, scalar2=None, op0=ALU.mult)
            pos = gw[b].rearrange("p w j t -> p (w j t)")
            neg = gn[b][:].rearrange("p w j t -> p (w j t)")
            for first, count in QCALLS:
                sign, w = SEQ[first]
                if sign > 0:
                    src = pos[:, 512 * w:512 * (w + count)]
                else:
                    src = neg[:, 512 * (w - 1):512 * (w - 1 + count)]
                cols = slice(P * first, P * (first + count))
                nc.vector.quantize_mx(out=wc[b][:, cols].bitcast(FP8X4), scales=ws[b][:, cols], in_=src)

        def x_transpose(r):
            words = xraw[r][:].bitcast(F32)
            for h in range(2):
                xt = ps.tile([P, 4, P], F32, name="xt", tag="bank")
                for t in range(4):
                    nc.tensor.transpose(xt[:, t, :], words[:, 2 * t + h:1024:8], ident[:])
                parted = xt[:].bitcast(BF16).rearrange("p t (n e) -> p e n t", e=2)
                if h == 1 and r in V_COPIES:
                    nc.vector.tensor_copy(out=gx[r][:, 2 * h:2 * h + 2, :, :], in_=parted)
                else:
                    nc.scalar.copy(out=gx[r][:, 2 * h:2 * h + 2, :, :], in_=parted)

        def x_quant(r):
            nc.vector.quantize_mx(
                out=xc[r][:].bitcast(FP8X4),
                scales=xs[r][:],
                in_=gx[r][:].rearrange("p c n t -> p (c n t)"),
            )

        res_of = {}

        def job(r, b, bias_sb):
            if b % 2 == 0:
                res = outp.tile([P, 1024], F32, name="res")
                f8 = outp.tile([P, 1024], FP8, name="f8")
                res_of[r] = (res, f8)
            res, f8 = res_of[r]
            acc = ps.tile([P, 512], F32, name="acc", tag="bank")
            for cp in range(2):
                for a in range(4):
                    wcols = slice(P * WIN[a][cp], P * (WIN[a][cp] + 2))
                    xcols = slice(P * a, P * (a + 1))
                    nc.tensor.matmul_mx(
                        out=acc[:, 256 * cp:256 * (cp + 1)],
                        lhsT=xc[r][:, xcols].bitcast(FP8X4),
                        lhsT_scale=xs[r][:, xcols],
                        rhs=wc[b][:, wcols].bitcast(FP8X4),
                        rhs_scale=ws[b][:, wcols],
                        start=(a == 0),
                        stop=(a == 3),
                    )
            cols = slice(512 * b, 512 * (b + 1))
            part = slice(512 * (b % 2), 512 * (b % 2 + 1))
            nc.vector.tensor_tensor(
                out=res[:, part].rearrange("p (j c) -> p j c", c=4),
                in0=acc[:].rearrange("p (c j) -> p j c", c=4),
                in1=bias_sb[:, cols].rearrange("p (j c) -> p j c", c=4),
                op=ALU.add,
            )
            nc.scalar.activation(out=f8[:, part], in_=res[:, part], func=ACT.Copy, scale=Y_SCALE, saturate=False)
            if b % 2 == 1:
                rows = slice(P * r, P * (r + 1))
                half = slice(512 * (b - 1), 512 * (b + 1))
                nc.scalar.dma_start(out=o0[rows, half], in_=res[:])
                nc.sync.dma_start(out=o1[rows, half], in_=f8[:].bitcast(U8))

        with tc.manual_schedule(engines={mybir.EngineType.PE}):
            for kind, idx in ORDER:
                if kind == "w":
                    w_transpose(idx)
                    if idx == 3:
                        w_quant(0)
                        w_quant(1)
                else:
                    x_transpose(idx)
                    if idx == 0:
                        x_quant(0)
            bias_sb = share.tile([P, 2048], BF16, name="bias_sb", tag="slot")
            nc.sync.dma_start(out=bias_sb[:], in_=bias.partition_broadcast(P))
            for r in range(1, ROW_TILES):
                x_quant(r)
            for pair in range(2):
                for r in range(ROW_TILES):
                    if pair == 0 and r == 2:
                        w_quant(2)
                    if pair == 0 and r == 5:
                        w_quant(3)
                    job(r, 2 * pair, bias_sb)
                    job(r, 2 * pair + 1, bias_sb)
